import numpy as np
import ml_dtypes


def mxq(x, axis, fmt="e4m3"):
    dtype, down = {"e4m3": (ml_dtypes.float8_e4m3fn, 7), "e5m2": (ml_dtypes.float8_e5m2, 14)}[fmt]
    v = np.moveaxis(np.asarray(x, np.float32).astype(ml_dtypes.bfloat16).astype(np.float64), axis, -1)
    blocks = v.reshape(v.shape[:-1] + (-1, 32))
    amax = np.abs(blocks).max(-1, keepdims=True)
    byte = np.maximum(np.where(amax > 0, np.frexp(amax)[1] - 1 + 127, 0) - down, 1)
    scale = np.exp2(byte - 127.0)
    codes = (blocks / scale).astype(np.float32).astype(dtype).astype(np.float64)
    return np.moveaxis((codes * scale).reshape(v.shape), -1, axis)


WIDE = False


def mx_kscale(k):
    if not WIDE:
        return np.ones(k)
    levels = np.array([10, -10, 5, -5, 0])
    if k % 512:
        return np.exp2(np.random.permutation(np.resize(levels, k // 32))).repeat(32)
    a = np.empty((k // 512, 16))
    for p in range(k // 512):
        a[p, :8] = np.random.permutation(np.resize(levels, 8))
        for g in range(8):
            far = levels[np.abs(levels - a[p, g]) >= 10]
            a[p, g + 8] = far[np.random.randint(len(far))]
    return np.exp2(a.ravel()).repeat(32)


BF16 = ml_dtypes.bfloat16


def bf(x):
    return np.asarray(x, np.float32).astype(BF16)


def f64(x):
    return np.asarray(x).astype(np.float64)


B, D, H = 1024, 512, 1024


def sigmoid(v):
    return 1.0 / (1.0 + np.exp(-v))


def setup_inputs():
    s = mx_kscale(B)[:, None]
    u = mx_kscale(H)
    x0 = bf(np.random.standard_normal((B, D)))
    w0 = bf(np.random.standard_normal((4 * H, D)) * 1.5 / np.sqrt(D))
    b_ih0 = bf(np.random.standard_normal(4 * H) * 0.3)
    b_hh0 = bf(np.random.standard_normal(4 * H) * 0.3)
    g = bf(np.random.standard_normal((B, H)) * np.exp2(np.random.randint(-6, 1, (B, 1))) * 8.0 / s * u[None, :])
    a = f64(x0) @ f64(w0).T + f64(b_ih0) + f64(b_hh0)
    div = np.concatenate([u, np.ones(H), u, u])
    return {"x": bf(f64(x0) * s),
            "W_ih0": bf(f64(w0) / div[:, None]),
            "b_ih0": b_ih0,
            "b_hh0": b_hh0,
            "a_i": np.asarray(a[:, :H], np.float32),
            "a_g": np.asarray(a[:, 2 * H:3 * H], np.float32),
            "a_o": np.asarray(a[:, 3 * H:], np.float32),
            "grad_out": g}


def reference(x, W_ih0, b_ih0, b_hh0, a_i, a_g, a_o, grad_out):
    w = f64(W_ih0)
    g = f64(grad_out)
    si = sigmoid(f64(a_i))
    tg = np.tanh(f64(a_g))
    so = sigmoid(f64(a_o))
    tc = np.tanh(si * tg)
    dc = g * so * (1.0 - tc * tc)
    da_i = dc * tg * si * (1.0 - si)
    da_g = dc * si * (1.0 - tg * tg)
    da_o = g * tc * so * (1.0 - so)
    da = np.concatenate([da_i, da_g, da_o], axis=1)
    wu = np.concatenate([w[:H], w[2 * H:]], axis=0)
    dx = mxq(da, 1, "e5m2") @ mxq(wu, 0, "e4m3")
    dwu = mxq(da, 0, "e5m2").T @ mxq(f64(x), 0, "e4m3")
    dw = np.concatenate([dwu[:H], np.zeros((H, D)), dwu[H:]], axis=0)
    return dx, dw

@@ -1,0 +1,334 @@
+from contextlib import ExitStack
+
+import concourse.mybir as mybir
+from concourse.masks import make_identity
+
+B, D, H = 1024, 512, 1024
+FLOPS = 2 * 2 * B * 3 * H * D
+BYTES = B * D * 2 + 3 * H * D * 2 + 3 * B * H * 4 + B * H * 2 + B * D * 4 + 4 * H * D * 4
+
+F32 = mybir.dt.float32
+BF16 = mybir.dt.bfloat16
+U32 = mybir.dt.uint32
+U8 = mybir.dt.uint8
+E4 = mybir.dt.float8_e4m3fn_x4
+E5 = mybir.dt.float8_e5m2_x4
+ACT = mybir.ActivationFunctionType
+ALU = mybir.AluOpType
+
+P = 128
+UW = 256
+NU = 8
+GATES = ("o", "i", "g")
+ROW0 = {"i": 0, "g": 2 * H, "o": 3 * H}
+
+PREP_LOAD = {-3: [("w", "o", 0)], -2: [("w", "i", 0), ("w", "g", 0)], 0: [("x", "x", 0)], 1: [("w", "o", 1)], 2: [("w", "i", 1)], 3: [("w", "g", 1)], 4: [("x", "x", 1)]}
+PREP_V = {-2: [("w", "o", 0)], -1: [("w", "i", 0), ("w", "g", 0)]}
+PREP_S = {0: [("x", "x", 0)], 1: [("w", "o", 1)], 2: [("w", "i", 1)], 3: [("w", "g", 1)], 4: [("x", "x", 1)]}
+
+
+def tile_lstmbaseline_pa_v_kernel(tc, x, W_ih0, b_ih0, b_hh0, a_i, a_g, a_o, grad_out, out_0, out_1):
+    nc = tc.nc
+    with ExitStack() as ctx:
+        const = ctx.enter_context(tc.tile_pool(name="const", bufs=1))
+        apool = ctx.enter_context(tc.tile_pool(name="apool", bufs=4))
+        gpool = ctx.enter_context(tc.tile_pool(name="gpool", bufs=2))
+        wpool = ctx.enter_context(tc.tile_pool(name="wpool", bufs=2))
+        dpool = ctx.enter_context(tc.tile_pool(name="dpool", bufs=2))
+        bpool = ctx.enter_context(tc.tile_pool(name="bpool", bufs=3))
+        keep = ctx.enter_context(tc.tile_pool(name="keep", bufs=1))
+        ppool = ctx.enter_context(tc.tile_pool(name="ppool", bufs=3))
+        spool = ctx.enter_context(tc.tile_pool(name="spool", bufs=6))
+        accp = ctx.enter_context(tc.psum_pool(name="accp", bufs=1))
+        work = ctx.enter_context(tc.psum_pool(name="work", bufs=4))
+        ctx.enter_context(tc.manual_schedule())
+
+        av = {
+            "i": a_i.rearrange("(g p j) w -> p g j w", g=2, j=4),
+            "g": a_g.rearrange("(g p j) w -> p g j w", g=2, j=4),
+            "o": a_o.rearrange("(g p j) w -> p g j w", g=2, j=4),
+        }
+        gv = grad_out.rearrange("(g p j) w -> p g j w", g=2, j=4)
+        xv = x.rearrange("(g p j) d -> p g j d", g=2, j=4)
+        o0v = out_0.rearrange("(g p j) d -> p g j d", g=2, j=4)
+
+        warm = const.tile([P, 8], F32, name="warm")
+        nc.vector.memset(warm[:], 0.0)
+        nc.scalar.activation(out=warm[:], in_=warm[:], func=ACT.Sigmoid)
+        zero = const.tile([P, 1024], F32, name="zero")
+        nc.vector.memset(zero[:], 0.0)
+        ident = const.tile([P, P], BF16, name="ident")
+        make_identity(nc, ident[:])
+
+        T = {}
+
+        def parts(u):
+            return u // 4, (u // 2) % 2, u % 2
+
+        def prep_load(key):
+            kind, gate, n = key
+            raw = ppool.tile([P, 4, D], BF16, name="raw", tag="raw")
+            if kind == "x":
+                nc.sync.dma_start(out=raw[:], in_=xv[:, n, :, :])
+            else:
+                r0 = ROW0[gate] + 512 * n
+                nc.sync.dma_start(out=raw[:], in_=W_ih0[r0:r0 + 512, :].rearrange("(q t) d -> q t d", t=4))
+            T[("raw", key)] = raw
+
+        def prep_copy(key, eng):
+            il = ppool.tile([P, D, 4], BF16, name="il", tag="il", align_bytes=64)
+            src = T[("raw", key)][:].rearrange("p t d -> p d t")
+            if eng == "v":
+                nc.vector.tensor_copy(out=il[:], in_=src)
+            else:
+                nc.scalar.copy(out=il[:], in_=src)
+            T[("il", key)] = il
+
+        def prep_quant(key):
+            nm = "%s%s%d" % key
+            codes = keep.tile([P, D], U32, name="c" + nm, align_bytes=64)
+            scales = keep.tile([P, D], U8, name="s" + nm, align_bytes=64)
+            nc.vector.quantize_mx(out=codes[:].bitcast(E4), scales=scales[:], in_=T[("il", key)][:].rearrange("p d t -> p (d t)"))
+            T[("c", key)] = codes
+            T[("s", key)] = scales
+
+        def load_unit(u):
+            g_, h, wq = parts(u)
+            lo = 512 * h + UW * wq
+            for gate in ("i", "g", "o"):
+                t = apool.tile([P, 4, UW], F32, name="a" + gate, tag="a" + gate)
+                nc.sync.dma_start(out=t[:], in_=av[gate][:, g_, :, lo:lo + UW])
+                T[("a" + gate, u)] = t
+                if gate == "g" and wq == 0:
+                    gt = gpool.tile([P, 4, 512], BF16, name="gt", tag="gt")
+                    nc.sync.dma_start(out=gt[:], in_=gv[:, g_, :, 512 * h:512 * h + 512])
+                    T[("gt", u // 2)] = gt
+
+        def s1(u):
+            nc.scalar.activation(out=T[("ai", u)][:], in_=T[("ai", u)][:], func=ACT.Sigmoid)
+            nc.scalar.activation(out=T[("ag", u)][:], in_=T[("ag", u)][:], func=ACT.Tanh)
+            nc.scalar.activation(out=T[("ao", u)][:], in_=T[("ao", u)][:], func=ACT.Sigmoid)
+
+        def v1(u):
+            wq = u % 2
+            c = wpool.tile([P, 4, UW], F32, name="c", tag="c")
+            nc.vector.tensor_tensor(out=c[:], in0=T[("ai", u)][:], in1=T[("ag", u)][:], op=ALU.mult)
+            gg = wpool.tile([P, 4, UW], F32, name="gg", tag="gg")
+            nc.vector.tensor_tensor(out=gg[:], in0=T[("ao", u)][:], in1=T[("gt", u // 2)][:, :, UW * wq:UW * wq + UW], op=ALU.mult)
+            T[("c", u)] = c
+            T[("gg", u)] = gg
+
+        def s2(u):
+            tcn = wpool.tile([P, 4, UW], F32, name="tcn", tag="tcn")
+            nc.scalar.activation(out=tcn[:], in_=T[("c", u)][:], func=ACT.Tanh, scale=-1.0)
+            sq = wpool.tile([P, 4, UW], F32, name="sq", tag="sq")
+            nc.scalar.activation(out=sq[:], in_=tcn[:], func=ACT.Square)
+            nc.scalar.activation(out=T[("ag", u)][:], in_=T[("ag", u)][:], func=ACT.Square)
+            T[("tcn", u)] = tcn
+            T[("sq", u)] = sq
+
+        def stt(out, in0, in1):
+            nc.vector.scalar_tensor_tensor(out=out, in0=in0, scalar=1.0, in1=in1, op0=ALU.subtract, op1=ALU.mult)
+
+        def v2(u):
+            stt(T[("c", u)][:], T[("ai", u)][:], T[("c", u)][:])
+            stt(T[("tcn", u)][:], T[("ao", u)][:], T[("tcn", u)][:])
+            stt(T[("sq", u)][:], T[("sq", u)][:], T[("gg", u)][:])
+            stt(T[("ag", u)][:], T[("ag", u)][:], T[("ai", u)][:])
+
+        FACT = {"o": ("tcn", "gg"), "i": ("c", "sq"), "g": ("ag", "sq")}
+
+        def v3(u, gate):
+            k, wq = u // 2, u % 2
+            if wq == 0:
+                T[("da", gate, k)] = dpool.tile([P, 512, 4], BF16, name="da" + gate, tag="da" + gate, align_bytes=64)
+            da = T[("da", gate, k)]
+            f0, f1 = FACT[gate]
+            nc.vector.tensor_tensor(
+                out=da[:, UW * wq:UW * wq + UW, :].rearrange("p (c i) j -> p c j i", i=4),
+                in0=T[(f0, u)][:].rearrange("p j (c i) -> p c j i", i=4),
+                in1=T[(f1, u)][:].rearrange("p j (c i) -> p c j i", i=4),
+                op=ALU.mult,
+            )
+
+        def qa(u, gate):
+            g_, h, wq = parts(u)
+            k = u // 2
+            if wq == 0:
+                nm = "%s%d" % (gate, k)
+                T[("cA", gate, k)] = keep.tile([P, 512], U32, name="cA" + nm, align_bytes=64)
+                T[("sA", gate, k)] = keep.tile([P, 512], U8, name="sA" + nm, align_bytes=64)
+            cols = slice(UW * wq, UW * wq + UW)
+            nc.vector.quantize_mx(
+                out=T[("cA", gate, k)][:, cols].bitcast(E5),
+                scales=T[("sA", gate, k)][:, cols],
+                in_=T[("da", gate, k)][:, cols, :].rearrange("p w j -> p (w j)"),
+            )
+
+        def tr(k, gate, jp):
+            view = T[("da", gate, k)][:].rearrange("p (q t) j -> p q t j", t=4)
+            tp = work.tile([P, 4, 256], BF16, name="tp", tag="work")
+            for j2 in range(2):
+                for t in range(4):
+                    nc.tensor.transpose(out=tp[:, t, P * j2:P * j2 + P], in_=view[:, :, t, 2 * jp + j2], identity=ident[:])
+            T[("tp", gate, k, jp)] = tp
+
+        def eb(k, gate, jp, eng):
+            if jp == 0:
+                T[("bt", gate, k)] = bpool.tile([P, 512, 4], BF16, name="bt", tag="bt", align_bytes=64)
+            dst = T[("bt", gate, k)][:, 256 * jp:256 * jp + 256, :]
+            src = T[("tp", gate, k, jp)][:].rearrange("q t c -> q c t")
+            if eng == "v":
+                nc.vector.tensor_copy(out=dst, in_=src)
+            else:
+                nc.scalar.copy(out=dst, in_=src)
+
+        def qb(k, gate, halves):
+            cB = bpool.tile([P, 512], U32, name="cB", tag="cB", align_bytes=64)
+            sB = bpool.tile([P, 512], U8, name="sB", tag="sB", align_bytes=64)
+            n = 512 // halves
+            for s in range(halves):
+                cols = slice(n * s, n * s + n)
+                nc.vector.quantize_mx(out=cB[:, cols].bitcast(E5), scales=sB[:, cols], in_=T[("bt", gate, k)][:, cols, :].rearrange("q c t -> q (c t)"))
+            T[("cB", gate, k)] = cB
+            T[("sB", gate, k)] = sB
+
+        def mm0(k, gate):
+            g_, h = k // 2, k % 2
+            key = ("w", gate, h)
+            for j in range(4):
+                if h == 0 and gate == GATES[0]:
+                    T[("acc", g_, j)] = accp.tile([P, D], F32, name="acc%d" % j, tag="acc%d" % j)
+                cols = slice(P * j, P * j + P)
+                nc.tensor.matmul_mx(
+                    out=T[("acc", g_, j)][:],
+                    lhsT=T[("cB", gate, k)][:, cols].bitcast(E5), lhsT_scale=T[("sB", gate, k)][:, cols],
+                    rhs=T[("c", key)][:].bitcast(E4), rhs_scale=T[("s", key)][:],
+                    start=(h == 0 and gate == GATES[0]), stop=(h == 1 and gate == GATES[2]),
+                )
+
+        def evac(src, dst_dram, eng):
+            st = spool.tile([P, D], F32, name="st", tag="st")
+            if eng == "v":
+                nc.vector.tensor_copy(out=st[:], in_=src)
+            else:
+                nc.scalar.copy(out=st[:], in_=src)
+            nc.sync.dma_start(out=dst_dram, in_=st[:])
+
+        def eo0(g_, j, eng):
+            evac(T[("acc", g_, j)][:], o0v[:, g_, j, :], eng)
+
+        def mm1(u, n):
+            g_, h, wq = parts(u)
+            gate, m = GATES[n // 2], 2 * wq + n % 2
+            acc = work.tile([P, D], F32, name="o1", tag="work")
+            cols = slice(P * m, P * m + P)
+            for gg_ in range(2):
+                k = 2 * gg_ + h
+                key = ("x", "x", gg_)
+                nc.tensor.matmul_mx(
+                    out=acc[:],
+                    lhsT=T[("cA", gate, k)][:, cols].bitcast(E5), lhsT_scale=T[("sA", gate, k)][:, cols],
+                    rhs=T[("c", key)][:].bitcast(E4), rhs_scale=T[("s", key)][:],
+                    start=(gg_ == 0), stop=(gg_ == 1),
+                )
+            T[("o1", u, n)] = acc
+
+        def eo1(u, n, eng):
+            g_, h, wq = parts(u)
+            gate, m = GATES[n // 2], 2 * wq + n % 2
+            r0 = ROW0[gate] + 512 * h + P * m
+            evac(T[("o1", u, n)][:], out_1[r0:r0 + P, :], eng)
+
+        PIECES = [(gate, jp) for gate in GATES for jp in range(2)]
+        for v in range(-3, NU):
+            um = v - 1
+            do1 = 4 <= um < NU
+            kb = (v - 2) // 2 if (v >= 2 and v % 2 == 0) else None
+            kq = (v - 3) // 2 if (v >= 3 and v % 2 == 1) else None
+            for key in PREP_LOAD.get(v, []):
+                prep_load(key)
+            if v + 3 < NU:
+                load_unit(v + 3)
+            if v == 1:
+                for z in range(4):
+                    nc.sync.dma_start(out=out_1[H + 256 * z:H + 256 * z + 256, :].rearrange("(p r) d -> p (r d)", r=2), in_=zero[:])
+            if 0 <= v + 2 < NU:
+                s1(v + 2)
+            for key in PREP_V.get(v, []):
+                prep_copy(key, "v")
+            if 0 <= v + 1 < NU:
+                v1(v + 1)
+            for key in PREP_V.get(v, []) + PREP_S.get(v - 1, []):
+                prep_quant(key)
+            if kq is not None:
+                for gate in GATES:
+                    qb(kq, gate, 1)
+            if do1:
+                for n in range(4):
+                    mm1(um, n)
+            if kq is not None:
+                for gate in GATES:
+                    mm0(kq, gate)
+            if do1:
+                eo1(um, 0, "s")
+                eo1(um, 1, "s")
+                mm1(um, 4)
+                mm1(um, 5)
+                eo1(um, 2, "s")
+                eo1(um, 3, "s")
+            if 0 <= v + 1 < NU:
+                s2(v + 1)
+            if do1:
+                eo1(um, 4, "s")
+                eo1(um, 5, "s")
+            if kq is not None and kq % 2 == 1:
+                for j in range(4):
+                    eo0(kq // 2, j, "s")
+            if kb is not None:
+                for n in range(4):
+                    tr(kb, PIECES[n][0], PIECES[n][1])
+                eb(kb, "o", 0, "s")
+                eb(kb, "o", 1, "s")
+                tr(kb, "g", 0)
+                tr(kb, "g", 1)
+                for n in range(2, 6):
+                    eb(kb, PIECES[n][0], PIECES[n][1], "s")
+            for key in PREP_S.get(v, []):
+                prep_copy(key, "s")
+            if 0 <= v < NU:
+                v2(v)
+                for gate in GATES:
+                    v3(v, gate)
+                    if v == NU - 1 and gate != "g":
+                        tr(v // 2, gate, 0)
+                        tr(v // 2, gate, 1)
+                for gate in GATES:
+                    qa(v, gate)
+        k, u = 3, NU - 1
+        eb(k, "o", 0, "s")
+        eb(k, "o", 1, "s")
+        tr(k, "g", 0)
+        tr(k, "g", 1)
+        eb(k, "i", 0, "s")
+        eb(k, "i", 1, "s")
+        qb(k, "o", 1)
+        mm0(k, "o")
+        mm1(u, 0)
+        mm1(u, 1)
+        qb(k, "i", 1)
+        mm0(k, "i")
+        eb(k, "g", 0, "s")
+        eb(k, "g", 1, "v")
+        qb(k, "g", 2)
+        mm0(k, "g")
+        mm1(u, 2)
+        mm1(u, 3)
+        eo1(u, 0, "s")
+        eo1(u, 1, "v")
+        mm1(u, 4)
+        mm1(u, 5)
+        for j in range(4):
+            eo0(1, j, "s" if j % 2 == 0 else "v")
+        for n in range(2, 6):
+            eo1(u, n, "s" if n % 2 == 0 else "v")

@@ -19,12 +19,11 @@ ALU = mybir.AluOpType
 P = 128
 UW = 256
 NU = 8
-GATES = ("o", "i", "g")
 ROW0 = {"i": 0, "g": 2 * H, "o": 3 * H}
+WORDS = True
+RUN = 2
 
-PREP_LOAD = {-3: [("w", "o", 0)], -2: [("w", "i", 0), ("w", "g", 0)], 0: [("x", "x", 0)], 1: [("w", "o", 1)], 2: [("w", "i", 1)], 3: [("w", "g", 1)], 4: [("x", "x", 1)]}
-PREP_V = {-2: [("w", "o", 0)], -1: [("w", "i", 0), ("w", "g", 0)]}
-PREP_S = {0: [("x", "x", 0)], 1: [("w", "o", 1)], 2: [("w", "i", 1)], 3: [("w", "g", 1)], 4: [("x", "x", 1)]}
+PREP = [("oi", 0), ("g", 0), ("oi", 1), ("oi", 2), ("g", 1), ("oi", 3), ("x", 0), ("x", 1)]
 
 
 def tile_lstmbaseline_pa_v_kernel(tc, x, W_ih0, b_ih0, b_hh0, a_i, a_g, a_o, grad_out, out_0, out_1):
@@ -37,8 +36,8 @@ def tile_lstmbaseline_pa_v_kernel(tc, x, W_ih0, b_ih0, b_hh0, a_i, a_g, a_o, gra
         dpool = ctx.enter_context(tc.tile_pool(name="dpool", bufs=2))
         bpool = ctx.enter_context(tc.tile_pool(name="bpool", bufs=3))
         keep = ctx.enter_context(tc.tile_pool(name="keep", bufs=1))
-        ppool = ctx.enter_context(tc.tile_pool(name="ppool", bufs=3))
-        spool = ctx.enter_context(tc.tile_pool(name="spool", bufs=6))
+        ppool = ctx.enter_context(tc.tile_pool(name="ppool", bufs=2))
+        spool = ctx.enter_context(tc.tile_pool(name="spool", bufs=10))
         accp = ctx.enter_context(tc.psum_pool(name="accp", bufs=1))
         work = ctx.enter_context(tc.psum_pool(name="work", bufs=4))
         ctx.enter_context(tc.manual_schedule())
@@ -52,43 +51,49 @@ def tile_lstmbaseline_pa_v_kernel(tc, x, W_ih0, b_ih0, b_hh0, a_i, a_g, a_o, gra
         xv = x.rearrange("(g p j) d -> p g j d", g=2, j=4)
         o0v = out_0.rearrange("(g p j) d -> p g j d", g=2, j=4)
 
-        warm = const.tile([P, 8], F32, name="warm")
-        nc.vector.memset(warm[:], 0.0)
-        nc.scalar.activation(out=warm[:], in_=warm[:], func=ACT.Sigmoid)
-        zero = const.tile([P, 1024], F32, name="zero")
-        nc.vector.memset(zero[:], 0.0)
-        ident = const.tile([P, P], BF16, name="ident")
-        make_identity(nc, ident[:])
-
         T = {}
 
         def parts(u):
             return u // 4, (u // 2) % 2, u % 2
 
+        warm = const.tile([P, 8], F32, name="warm")
+        nc.vector.memset(warm[:], 0.0)
+        nc.scalar.activation(out=warm[:], in_=warm[:], func=ACT.Sigmoid)
+        zero = const.tile([P, 1024], F32, name="zero")
+        nc.vector.memset(zero[:], 0.0)
+        identb = const.tile([P, P], BF16, name="identb")
+        make_identity(nc, identb[:])
+        identf = const.tile([P, P], F32, name="identf")
+        make_identity(nc, identf[:])
+
         def prep_load(key):
-            kind, gate, n = key
-            raw = ppool.tile([P, 4, D], BF16, name="raw", tag="raw")
+            kind, n = key
+            raw = ppool.tile([P, 4, D], BF16, name="raw", tag="raw", bufs=3)
             if kind == "x":
                 nc.sync.dma_start(out=raw[:], in_=xv[:, n, :, :])
-            else:
-                r0 = ROW0[gate] + 512 * n
+            elif kind == "g":
+                r0 = ROW0["g"] + 512 * n
                 nc.sync.dma_start(out=raw[:], in_=W_ih0[r0:r0 + 512, :].rearrange("(q t) d -> q t d", t=4))
+            else:
+                for s, gate in enumerate(("o", "i")):
+                    r0 = ROW0[gate] + UW * n
+                    nc.sync.dma_start(out=raw[64 * s:64 * s + 64, :, :], in_=W_ih0[r0:r0 + UW, :].rearrange("(q t) d -> q t d", t=4))
             T[("raw", key)] = raw
 
-        def prep_copy(key, eng):
-            il = ppool.tile([P, D, 4], BF16, name="il", tag="il", align_bytes=64)
-            src = T[("raw", key)][:].rearrange("p t d -> p d t")
-            if eng == "v":
-                nc.vector.tensor_copy(out=il[:], in_=src)
-            else:
-                nc.scalar.copy(out=il[:], in_=src)
-            T[("il", key)] = il
+        def prep_move(key, s):
+            if s == 0:
+                T[("il", key)] = ppool.tile([P, 4 * D], BF16, name="il", tag="il", align_bytes=64)
+            pp = work.tile([P, 1024], BF16, name="pp", tag="work")
+            for r in range(2):
+                d0 = 256 * s + 128 * r
+                nc.tensor.matmul(out=pp[:, 512 * r:512 * r + 512].rearrange("p (d t) -> p d t", t=4), lhsT=identb[:], rhs=T[("raw", key)][:, :, d0:d0 + 128].rearrange("p t d -> p d t"), start=True, stop=True)
+            nc.scalar.copy(out=T[("il", key)][:, 1024 * s:1024 * s + 1024], in_=pp[:])
 
         def prep_quant(key):
-            nm = "%s%s%d" % key
+            nm = "%s%d" % key
             codes = keep.tile([P, D], U32, name="c" + nm, align_bytes=64)
             scales = keep.tile([P, D], U8, name="s" + nm, align_bytes=64)
-            nc.vector.quantize_mx(out=codes[:].bitcast(E4), scales=scales[:], in_=T[("il", key)][:].rearrange("p d t -> p (d t)"))
+            nc.vector.quantize_mx(out=codes[:].bitcast(E4), scales=scales[:], in_=T[("il", key)][:])
             T[("c", key)] = codes
             T[("s", key)] = scales
 
@@ -99,10 +104,10 @@ def tile_lstmbaseline_pa_v_kernel(tc, x, W_ih0, b_ih0, b_hh0, a_i, a_g, a_o, gra
                 t = apool.tile([P, 4, UW], F32, name="a" + gate, tag="a" + gate)
                 nc.sync.dma_start(out=t[:], in_=av[gate][:, g_, :, lo:lo + UW])
                 T[("a" + gate, u)] = t
-                if gate == "g" and wq == 0:
-                    gt = gpool.tile([P, 4, 512], BF16, name="gt", tag="gt")
-                    nc.sync.dma_start(out=gt[:], in_=gv[:, g_, :, 512 * h:512 * h + 512])
-                    T[("gt", u // 2)] = gt
+            if wq == 0:
+                gt = gpool.tile([P, 4, 512], BF16, name="gt", tag="gt")
+                nc.sync.dma_start(out=gt[:], in_=gv[:, g_, :, 512 * h:512 * h + 512])
+                T[("gt", u // 2)] = gt
 
         def s1(u):
             nc.scalar.activation(out=T[("ai", u)][:], in_=T[("ai", u)][:], func=ACT.Sigmoid)
@@ -130,81 +135,105 @@ def tile_lstmbaseline_pa_v_kernel(tc, x, W_ih0, b_ih0, b_hh0, a_i, a_g, a_o, gra
         def stt(out, in0, in1):
             nc.vector.scalar_tensor_tensor(out=out, in0=in0, scalar=1.0, in1=in1, op0=ALU.subtract, op1=ALU.mult)
 
-        def v2(u):
-            stt(T[("c", u)][:], T[("ai", u)][:], T[("c", u)][:])
-            stt(T[("tcn", u)][:], T[("ao", u)][:], T[("tcn", u)][:])
-            stt(T[("sq", u)][:], T[("sq", u)][:], T[("gg", u)][:])
-            stt(T[("ag", u)][:], T[("ag", u)][:], T[("ai", u)][:])
+        def v2(u, names):
+            for nm in names:
+                if nm == "c":
+                    stt(T[("c", u)][:], T[("ai", u)][:], T[("c", u)][:])
+                elif nm == "tcn":
+                    stt(T[("tcn", u)][:], T[("ao", u)][:], T[("tcn", u)][:])
+                elif nm == "sq":
+                    stt(T[("sq", u)][:], T[("sq", u)][:], T[("gg", u)][:])
+                else:
+                    stt(T[("ag", u)][:], T[("ag", u)][:], T[("ai", u)][:])
 
         FACT = {"o": ("tcn", "gg"), "i": ("c", "sq"), "g": ("ag", "sq")}
 
         def v3(u, gate):
             k, wq = u // 2, u % 2
-            if wq == 0:
-                T[("da", gate, k)] = dpool.tile([P, 512, 4], BF16, name="da" + gate, tag="da" + gate, align_bytes=64)
-            da = T[("da", gate, k)]
+            if gate == "g":
+                if wq == 0:
+                    T[("da", "g", k)] = dpool.tile([P, 512, 4], BF16, name="dag", tag="dag", align_bytes=64)
+                da, lo = T[("da", "g", k)], UW * wq
+            else:
+                if ("da", "oi", u) not in T:
+                    T[("da", "oi", u)] = dpool.tile([P, 512, 4], BF16, name="daoi", tag="daoi", align_bytes=64)
+                da, lo = T[("da", "oi", u)], (0 if gate == "o" else UW)
             f0, f1 = FACT[gate]
             nc.vector.tensor_tensor(
-                out=da[:, UW * wq:UW * wq + UW, :].rearrange("p (c i) j -> p c j i", i=4),
-                in0=T[(f0, u)][:].rearrange("p j (c i) -> p c j i", i=4),
-                in1=T[(f1, u)][:].rearrange("p j (c i) -> p c j i", i=4),
+                out=da[:, lo:lo + UW, :].rearrange("p (c i) j -> p c j i", i=RUN),
+                in0=T[(f0, u)][:].rearrange("p j (c i) -> p c j i", i=RUN),
+                in1=T[(f1, u)][:].rearrange("p j (c i) -> p c j i", i=RUN),
                 op=ALU.mult,
             )
 
-        def qa(u, gate):
-            g_, h, wq = parts(u)
-            k = u // 2
-            if wq == 0:
-                nm = "%s%d" % (gate, k)
-                T[("cA", gate, k)] = keep.tile([P, 512], U32, name="cA" + nm, align_bytes=64)
-                T[("sA", gate, k)] = keep.tile([P, 512], U8, name="sA" + nm, align_bytes=64)
-            cols = slice(UW * wq, UW * wq + UW)
+        def qa(u, kind):
+            k, wq = u // 2, u % 2
+            if kind == "oi":
+                T[("cA", "oi", u)] = keep.tile([P, 512], U32, name="cAoi%d" % u, align_bytes=64)
+                T[("sA", "oi", u)] = keep.tile([P, 512], U8, name="sAoi%d" % u, align_bytes=64)
+                n, cols = u, slice(0, 512)
+            else:
+                if wq == 0:
+                    T[("cA", "g", k)] = keep.tile([P, 512], U32, name="cAg%d" % k, align_bytes=64)
+                    T[("sA", "g", k)] = keep.tile([P, 512], U8, name="sAg%d" % k, align_bytes=64)
+                n, cols = k, slice(UW * wq, UW * wq + UW)
             nc.vector.quantize_mx(
-                out=T[("cA", gate, k)][:, cols].bitcast(E5),
-                scales=T[("sA", gate, k)][:, cols],
-                in_=T[("da", gate, k)][:, cols, :].rearrange("p w j -> p (w j)"),
+                out=T[("cA", kind, n)][:, cols].bitcast(E5),
+                scales=T[("sA", kind, n)][:, cols],
+                in_=T[("da", kind, n)][:, cols, :].rearrange("p w j -> p (w j)"),
             )
 
-        def tr(k, gate, jp):
-            view = T[("da", gate, k)][:].rearrange("p (q t) j -> p q t j", t=4)
-            tp = work.tile([P, 4, 256], BF16, name="tp", tag="work")
-            for j2 in range(2):
+        def tr(ps, s):
+            da = T[("da", ps[0], ps[1])]
+            if WORDS:
+                words = da[:].rearrange("p w j -> p (w j)").bitcast(F32).rearrange("p (q r) -> p q r", r=8)
+                tp = work.tile([P, 4, P], F32, name="tp", tag="work")
                 for t in range(4):
-                    nc.tensor.transpose(out=tp[:, t, P * j2:P * j2 + P], in_=view[:, :, t, 2 * jp + j2], identity=ident[:])
-            T[("tp", gate, k, jp)] = tp
+                    nc.tensor.transpose(out=tp[:, t, :], in_=words[:, :, 2 * t + s], identity=identf[:])
+            else:
+                view = da[:].rearrange("p (q t) j -> p q t j", t=4)
+                tp = work.tile([P, 4, 256], BF16, name="tp", tag="work")
+                for j2 in range(2):
+                    for t in range(4):
+                        nc.tensor.transpose(out=tp[:, t, P * j2:P * j2 + P], in_=view[:, :, t, 2 * s + j2], identity=identb[:])
+            T[("tp", ps, s)] = tp
 
-        def eb(k, gate, jp, eng):
-            if jp == 0:
-                T[("bt", gate, k)] = bpool.tile([P, 512, 4], BF16, name="bt", tag="bt", align_bytes=64)
-            dst = T[("bt", gate, k)][:, 256 * jp:256 * jp + 256, :]
-            src = T[("tp", gate, k, jp)][:].rearrange("q t c -> q c t")
+        def eb(ps, s, eng):
+            if s == 0:
+                T[("bt", ps)] = bpool.tile([P, 512, 4], BF16, name="bt", tag="bt", align_bytes=64)
+            if WORDS:
+                dst = T[("bt", ps)][:, 256 * s:256 * s + 256, :].rearrange("q (e c) t -> q e c t", e=2)
+                src = T[("tp", ps, s)][:].rearrange("q t c -> q (t c)").bitcast(BF16).rearrange("q (t c e) -> q e c t", t=4, e=2)
+            else:
+                dst = T[("bt", ps)][:, 256 * s:256 * s + 256, :]
+                src = T[("tp", ps, s)][:].rearrange("q t c -> q c t")
             if eng == "v":
                 nc.vector.tensor_copy(out=dst, in_=src)
             else:
                 nc.scalar.copy(out=dst, in_=src)
 
-        def qb(k, gate, halves):
+        def qb(ps, halves):
             cB = bpool.tile([P, 512], U32, name="cB", tag="cB", align_bytes=64)
             sB = bpool.tile([P, 512], U8, name="sB", tag="sB", align_bytes=64)
             n = 512 // halves
             for s in range(halves):
                 cols = slice(n * s, n * s + n)
-                nc.vector.quantize_mx(out=cB[:, cols].bitcast(E5), scales=sB[:, cols], in_=T[("bt", gate, k)][:, cols, :].rearrange("q c t -> q (c t)"))
-            T[("cB", gate, k)] = cB
-            T[("sB", gate, k)] = sB
+                nc.vector.quantize_mx(out=cB[:, cols].bitcast(E5), scales=sB[:, cols], in_=T[("bt", ps)][:, cols, :].rearrange("q c t -> q (c t)"))
+            T[("cB", ps)] = cB
+            T[("sB", ps)] = sB
 
-        def mm0(k, gate):
-            g_, h = k // 2, k % 2
-            key = ("w", gate, h)
+        def mm0(ps, first, last):
+            g_ = ps[1] // 4 if ps[0] == "oi" else ps[1] // 2
+            key = (ps[0], ps[1] % 4 if ps[0] == "oi" else ps[1] % 2)
             for j in range(4):
-                if h == 0 and gate == GATES[0]:
+                if first:
                     T[("acc", g_, j)] = accp.tile([P, D], F32, name="acc%d" % j, tag="acc%d" % j)
                 cols = slice(P * j, P * j + P)
                 nc.tensor.matmul_mx(
                     out=T[("acc", g_, j)][:],
-                    lhsT=T[("cB", gate, k)][:, cols].bitcast(E5), lhsT_scale=T[("sB", gate, k)][:, cols],
+                    lhsT=T[("cB", ps)][:, cols].bitcast(E5), lhsT_scale=T[("sB", ps)][:, cols],
                     rhs=T[("c", key)][:].bitcast(E4), rhs_scale=T[("s", key)][:],
-                    start=(h == 0 and gate == GATES[0]), stop=(h == 1 and gate == GATES[2]),
+                    start=first, stop=last,
                 )
 
         def evac(src, dst_dram, eng):
@@ -220,15 +249,17 @@ def tile_lstmbaseline_pa_v_kernel(tc, x, W_ih0, b_ih0, b_hh0, a_i, a_g, a_o, gra
 
         def mm1(u, n):
             g_, h, wq = parts(u)
-            gate, m = GATES[n // 2], 2 * wq + n % 2
             acc = work.tile([P, D], F32, name="o1", tag="work")
-            cols = slice(P * m, P * m + P)
             for gg_ in range(2):
-                k = 2 * gg_ + h
-                key = ("x", "x", gg_)
+                if n < 4:
+                    kind, idx, c0 = "oi", 4 * gg_ + u % 4, P * n
+                else:
+                    kind, idx, c0 = "g", 2 * gg_ + h, UW * wq + P * (n - 4)
+                cols = slice(c0, c0 + P)
+                key = ("x", gg_)
                 nc.tensor.matmul_mx(
                     out=acc[:],
-                    lhsT=T[("cA", gate, k)][:, cols].bitcast(E5), lhsT_scale=T[("sA", gate, k)][:, cols],
+                    lhsT=T[("cA", kind, idx)][:, cols].bitcast(E5), lhsT_scale=T[("sA", kind, idx)][:, cols],
                     rhs=T[("c", key)][:].bitcast(E4), rhs_scale=T[("s", key)][:],
                     start=(gg_ == 0), stop=(gg_ == 1),
                 )
@@ -236,99 +267,118 @@ def tile_lstmbaseline_pa_v_kernel(tc, x, W_ih0, b_ih0, b_hh0, a_i, a_g, a_o, gra
 
         def eo1(u, n, eng):
             g_, h, wq = parts(u)
-            gate, m = GATES[n // 2], 2 * wq + n % 2
-            r0 = ROW0[gate] + 512 * h + P * m
+            gate = ("o", "i", "g")[n // 2]
+            r0 = ROW0[gate] + 512 * h + UW * wq + P * (n % 2)
             evac(T[("o1", u, n)][:], out_1[r0:r0 + P, :], eng)
 
-        PIECES = [(gate, jp) for gate in GATES for jp in range(2)]
-        for v in range(-3, NU):
+        def passes_of(u):
+            if u % 2 == 0:
+                return [("oi", u)]
+            return [("g", u // 2), ("oi", u)]
+
+        def flags(ps):
+            first = ps[0] == "oi" and ps[1] % 4 == 0
+            last = ps[0] == "oi" and ps[1] % 4 == 3
+            return first, last
+
+        load_unit(0)
+        load_unit(1)
+        load_unit(2)
+        s1(0)
+        v1(0)
+        s2(0)
+        s1(1)
+        for v in range(0, NU):
             um = v - 1
-            do1 = 4 <= um < NU
-            kb = (v - 2) // 2 if (v >= 2 and v % 2 == 0) else None
-            kq = (v - 3) // 2 if (v >= 3 and v % 2 == 1) else None
-            for key in PREP_LOAD.get(v, []):
+            do1 = 4 <= um
+            pl = [PREP[n] for n in (2 * v, 2 * v + 1) if n < len(PREP)]
+            for key in pl:
                 prep_load(key)
             if v + 3 < NU:
                 load_unit(v + 3)
-            if v == 1:
+            if v == 2:
                 for z in range(4):
                     nc.sync.dma_start(out=out_1[H + 256 * z:H + 256 * z + 256, :].rearrange("(p r) d -> p (r d)", r=2), in_=zero[:])
-            if 0 <= v + 2 < NU:
+            bps = passes_of(um) if um >= 0 else []
+            for ps in bps:
+                eb(ps, 0, "s")
+                eb(ps, 1, "s")
+            if v + 2 < NU:
                 s1(v + 2)
-            for key in PREP_V.get(v, []):
-                prep_copy(key, "v")
-            if 0 <= v + 1 < NU:
+            if 1 <= v and v + 1 < NU:
                 v1(v + 1)
-            for key in PREP_V.get(v, []) + PREP_S.get(v - 1, []):
+            pq = [PREP[n] for n in (2 * v - 2, 2 * v - 1) if 0 <= n < len(PREP)]
+            for key in pq:
                 prep_quant(key)
-            if kq is not None:
-                for gate in GATES:
-                    qb(kq, gate, 1)
             if do1:
                 for n in range(4):
                     mm1(um, n)
-            if kq is not None:
-                for gate in GATES:
-                    mm0(kq, gate)
-            if do1:
                 eo1(um, 0, "s")
                 eo1(um, 1, "s")
                 mm1(um, 4)
                 mm1(um, 5)
                 eo1(um, 2, "s")
                 eo1(um, 3, "s")
-            if 0 <= v + 1 < NU:
+            if 1 <= v and v + 1 < NU:
                 s2(v + 1)
             if do1:
                 eo1(um, 4, "s")
                 eo1(um, 5, "s")
-            if kq is not None and kq % 2 == 1:
-                for j in range(4):
-                    eo0(kq // 2, j, "s")
-            if kb is not None:
-                for n in range(4):
-                    tr(kb, PIECES[n][0], PIECES[n][1])
-                eb(kb, "o", 0, "s")
-                eb(kb, "o", 1, "s")
-                tr(kb, "g", 0)
-                tr(kb, "g", 1)
-                for n in range(2, 6):
-                    eb(kb, PIECES[n][0], PIECES[n][1], "s")
-            for key in PREP_S.get(v, []):
-                prep_copy(key, "s")
-            if 0 <= v < NU:
-                v2(v)
-                for gate in GATES:
-                    v3(v, gate)
-                    if v == NU - 1 and gate != "g":
-                        tr(v // 2, gate, 0)
-                        tr(v // 2, gate, 1)
-                for gate in GATES:
-                    qa(v, gate)
-        k, u = 3, NU - 1
-        eb(k, "o", 0, "s")
-        eb(k, "o", 1, "s")
-        tr(k, "g", 0)
-        tr(k, "g", 1)
-        eb(k, "i", 0, "s")
-        eb(k, "i", 1, "s")
-        qb(k, "o", 1)
-        mm0(k, "o")
+            for key in pl:
+                prep_move(key, 0)
+                prep_move(key, 1)
+            v2(v, ("sq", "ag", "c") if v == NU - 1 else ("c", "tcn", "sq", "ag"))
+            for ps in bps:
+                qb(ps, 1)
+                mm0(ps, flags(ps)[0], flags(ps)[1])
+                if flags(ps)[1]:
+                    for j in range(4):
+                        eo0(ps[1] // 4, j, "s")
+            if v < NU - 1:
+                v3(v, "g")
+                if v % 2 == 1:
+                    tr(("g", v // 2), 0)
+                    tr(("g", v // 2), 1)
+                v3(v, "o")
+                v3(v, "i")
+                tr(("oi", v), 0)
+                tr(("oi", v), 1)
+                qa(v, "g")
+                qa(v, "oi")
+                if v == 0:
+                    v1(1)
+                    s2(1)
+        u = NU - 1
+        pg, po = ("g", 3), ("oi", 7)
+        v3(u, "g")
+        tr(pg, 0)
+        tr(pg, 1)
+        v2(u, ("tcn",))
+        v3(u, "i")
+        qa(u, "g")
+        mm1(u, 4)
+        mm1(u, 5)
+        eb(pg, 0, "s")
+        eb(pg, 1, "s")
+        v3(u, "o")
+        tr(po, 0)
+        tr(po, 1)
+        qb(pg, 1)
+        mm0(pg, False, False)
+        qa(u, "oi")
+        eo1(u, 4, "s")
+        eo1(u, 5, "v")
         mm1(u, 0)
         mm1(u, 1)
-        qb(k, "i", 1)
-        mm0(k, "i")
-        eb(k, "g", 0, "s")
-        eb(k, "g", 1, "v")
-        qb(k, "g", 2)
-        mm0(k, "g")
+        eb(po, 0, "s")
+        eb(po, 1, "v")
+        qb(po, 2)
+        mm0(po, False, True)
         mm1(u, 2)
         mm1(u, 3)
         eo1(u, 0, "s")
         eo1(u, 1, "v")
-        mm1(u, 4)
-        mm1(u, 5)
         for j in range(4):
             eo0(1, j, "s" if j % 2 == 0 else "v")
-        for n in range(2, 6):
-            eo1(u, n, "s" if n % 2 == 0 else "v")
+        eo1(u, 2, "s")
+        eo1(u, 3, "v")

@@ -22,6 +22,7 @@ NU = 8
 ROW0 = {"i": 0, "g": 2 * H, "o": 3 * H}
 WORDS = True
 RUN = 2
+HEAD_CUTS = 1
 
 PREP = [("oi", 0), ("g", 0), ("oi", 1), ("oi", 2), ("g", 1), ("oi", 3), ("x", 0), ("x", 1)]
 
@@ -37,7 +38,7 @@ def tile_lstmbaseline_pa_v_kernel(tc, x, W_ih0, b_ih0, b_hh0, a_i, a_g, a_o, gra
         bpool = ctx.enter_context(tc.tile_pool(name="bpool", bufs=3))
         keep = ctx.enter_context(tc.tile_pool(name="keep", bufs=1))
         ppool = ctx.enter_context(tc.tile_pool(name="ppool", bufs=2))
-        spool = ctx.enter_context(tc.tile_pool(name="spool", bufs=10))
+        spool = ctx.enter_context(tc.tile_pool(name="spool", bufs=8))
         accp = ctx.enter_context(tc.psum_pool(name="accp", bufs=1))
         work = ctx.enter_context(tc.psum_pool(name="work", bufs=4))
         ctx.enter_context(tc.manual_schedule())
@@ -82,7 +83,7 @@ def tile_lstmbaseline_pa_v_kernel(tc, x, W_ih0, b_ih0, b_hh0, a_i, a_g, a_o, gra
 
         def prep_move(key, s):
             if s == 0:
-                T[("il", key)] = ppool.tile([P, 4 * D], BF16, name="il", tag="il", align_bytes=64)
+                T[("il", key)] = ppool.tile([P, 4 * D], BF16, name="il", tag="il", bufs=4, align_bytes=64)
             pp = work.tile([P, 1024], BF16, name="pp", tag="work")
             for r in range(2):
                 d0 = 256 * s + 128 * r
@@ -97,27 +98,35 @@ def tile_lstmbaseline_pa_v_kernel(tc, x, W_ih0, b_ih0, b_hh0, a_i, a_g, a_o, gra
             T[("c", key)] = codes
             T[("s", key)] = scales
 
+        def jcuts(u):
+            n = HEAD_CUTS if u == 0 else 1
+            return [(4 // n * s, 4 // n * s + 4 // n) for s in range(n)]
+
         def load_unit(u):
             g_, h, wq = parts(u)
             lo = 512 * h + UW * wq
             for gate in ("i", "g", "o"):
-                t = apool.tile([P, 4, UW], F32, name="a" + gate, tag="a" + gate)
-                nc.sync.dma_start(out=t[:], in_=av[gate][:, g_, :, lo:lo + UW])
-                T[("a" + gate, u)] = t
+                T[("a" + gate, u)] = apool.tile([P, 4, UW], F32, name="a" + gate, tag="a" + gate)
+            for j0, j1 in jcuts(u):
+                for gate in ("i", "g"):
+                    nc.sync.dma_start(out=T[("a" + gate, u)][:, j0:j1, :], in_=av[gate][:, g_, j0:j1, lo:lo + UW])
+            nc.sync.dma_start(out=T[("ao", u)][:], in_=av["o"][:, g_, :, lo:lo + UW])
             if wq == 0:
                 gt = gpool.tile([P, 4, 512], BF16, name="gt", tag="gt")
                 nc.sync.dma_start(out=gt[:], in_=gv[:, g_, :, 512 * h:512 * h + 512])
                 T[("gt", u // 2)] = gt
 
         def s1(u):
-            nc.scalar.activation(out=T[("ai", u)][:], in_=T[("ai", u)][:], func=ACT.Sigmoid)
-            nc.scalar.activation(out=T[("ag", u)][:], in_=T[("ag", u)][:], func=ACT.Tanh)
+            for j0, j1 in jcuts(u):
+                nc.scalar.activation(out=T[("ai", u)][:, j0:j1, :], in_=T[("ai", u)][:, j0:j1, :], func=ACT.Sigmoid)
+                nc.scalar.activation(out=T[("ag", u)][:, j0:j1, :], in_=T[("ag", u)][:, j0:j1, :], func=ACT.Tanh)
             nc.scalar.activation(out=T[("ao", u)][:], in_=T[("ao", u)][:], func=ACT.Sigmoid)
 
         def v1(u):
             wq = u % 2
             c = wpool.tile([P, 4, UW], F32, name="c", tag="c")
-            nc.vector.tensor_tensor(out=c[:], in0=T[("ai", u)][:], in1=T[("ag", u)][:], op=ALU.mult)
+            for j0, j1 in jcuts(u):
+                nc.vector.tensor_tensor(out=c[:, j0:j1, :], in0=T[("ai", u)][:, j0:j1, :], in1=T[("ag", u)][:, j0:j1, :], op=ALU.mult)
             gg = wpool.tile([P, 4, UW], F32, name="gg", tag="gg")
             nc.vector.tensor_tensor(out=gg[:], in0=T[("ao", u)][:], in1=T[("gt", u // 2)][:, :, UW * wq:UW * wq + UW], op=ALU.mult)
             T[("c", u)] = c
@@ -125,7 +134,8 @@ def tile_lstmbaseline_pa_v_kernel(tc, x, W_ih0, b_ih0, b_hh0, a_i, a_g, a_o, gra
 
         def s2(u):
             tcn = wpool.tile([P, 4, UW], F32, name="tcn", tag="tcn")
-            nc.scalar.activation(out=tcn[:], in_=T[("c", u)][:], func=ACT.Tanh, scale=-1.0)
+            for j0, j1 in jcuts(u):
+                nc.scalar.activation(out=tcn[:, j0:j1, :], in_=T[("c", u)][:, j0:j1, :], func=ACT.Tanh, scale=-1.0)
             sq = wpool.tile([P, 4, UW], F32, name="sq", tag="sq")
             nc.scalar.activation(out=sq[:], in_=tcn[:], func=ACT.Square)
             nc.scalar.activation(out=T[("ag", u)][:], in_=T[("ag", u)][:], func=ACT.Square)
@@ -148,7 +158,7 @@ def tile_lstmbaseline_pa_v_kernel(tc, x, W_ih0, b_ih0, b_hh0, a_i, a_g, a_o, gra
 
         FACT = {"o": ("tcn", "gg"), "i": ("c", "sq"), "g": ("ag", "sq")}
 
-        def v3(u, gate):
+        def v3(u, gate, f0=0, fw=UW):
             k, wq = u // 2, u % 2
             if gate == "g":
                 if wq == 0:
@@ -158,20 +168,21 @@ def tile_lstmbaseline_pa_v_kernel(tc, x, W_ih0, b_ih0, b_hh0, a_i, a_g, a_o, gra
                 if ("da", "oi", u) not in T:
                     T[("da", "oi", u)] = dpool.tile([P, 512, 4], BF16, name="daoi", tag="daoi", align_bytes=64)
                 da, lo = T[("da", "oi", u)], (0 if gate == "o" else UW)
-            f0, f1 = FACT[gate]
+            n0, n1 = FACT[gate]
             nc.vector.tensor_tensor(
-                out=da[:, lo:lo + UW, :].rearrange("p (c i) j -> p c j i", i=RUN),
-                in0=T[(f0, u)][:].rearrange("p j (c i) -> p c j i", i=RUN),
-                in1=T[(f1, u)][:].rearrange("p j (c i) -> p c j i", i=RUN),
+                out=da[:, lo + f0:lo + f0 + fw, :].rearrange("p (c i) j -> p c j i", i=RUN),
+                in0=T[(n0, u)][:, :, f0:f0 + fw].rearrange("p j (c i) -> p c j i", i=RUN),
+                in1=T[(n1, u)][:, :, f0:f0 + fw].rearrange("p j (c i) -> p c j i", i=RUN),
                 op=ALU.mult,
             )
 
-        def qa(u, kind):
+        def qa(u, kind, c0=0, cw=512):
             k, wq = u // 2, u % 2
             if kind == "oi":
-                T[("cA", "oi", u)] = keep.tile([P, 512], U32, name="cAoi%d" % u, align_bytes=64)
-                T[("sA", "oi", u)] = keep.tile([P, 512], U8, name="sAoi%d" % u, align_bytes=64)
-                n, cols = u, slice(0, 512)
+                if ("cA", "oi", u) not in T:
+                    T[("cA", "oi", u)] = keep.tile([P, 512], U32, name="cAoi%d" % u, align_bytes=64)
+                    T[("sA", "oi", u)] = keep.tile([P, 512], U8, name="sAoi%d" % u, align_bytes=64)
+                n, cols = u, slice(c0, c0 + cw)
             else:
                 if wq == 0:
                     T[("cA", "g", k)] = keep.tile([P, 512], U32, name="cAg%d" % k, align_bytes=64)
@@ -198,12 +209,15 @@ def tile_lstmbaseline_pa_v_kernel(tc, x, W_ih0, b_ih0, b_hh0, a_i, a_g, a_o, gra
                         nc.tensor.transpose(out=tp[:, t, P * j2:P * j2 + P], in_=view[:, :, t, 2 * s + j2], identity=identb[:])
             T[("tp", ps, s)] = tp
 
-        def eb(ps, s, eng):
-            if s == 0:
+        def eb(ps, s, eng, par=None):
+            if ("bt", ps) not in T:
                 T[("bt", ps)] = bpool.tile([P, 512, 4], BF16, name="bt", tag="bt", align_bytes=64)
             if WORDS:
                 dst = T[("bt", ps)][:, 256 * s:256 * s + 256, :].rearrange("q (e c) t -> q e c t", e=2)
                 src = T[("tp", ps, s)][:].rearrange("q t c -> q (t c)").bitcast(BF16).rearrange("q (t c e) -> q e c t", t=4, e=2)
+                if par is not None:
+                    dst = dst[:, par, :, :]
+                    src = src[:, par, :, :]
             else:
                 dst = T[("bt", ps)][:, 256 * s:256 * s + 256, :]
                 src = T[("tp", ps, s)][:].rearrange("q t c -> q c t")
@@ -212,20 +226,17 @@ def tile_lstmbaseline_pa_v_kernel(tc, x, W_ih0, b_ih0, b_hh0, a_i, a_g, a_o, gra
             else:
                 nc.scalar.copy(out=dst, in_=src)
 
-        def qb(ps, halves):
-            cB = bpool.tile([P, 512], U32, name="cB", tag="cB", align_bytes=64)
-            sB = bpool.tile([P, 512], U8, name="sB", tag="sB", align_bytes=64)
-            n = 512 // halves
-            for s in range(halves):
-                cols = slice(n * s, n * s + n)
-                nc.vector.quantize_mx(out=cB[:, cols].bitcast(E5), scales=sB[:, cols], in_=T[("bt", ps)][:, cols, :].rearrange("q c t -> q (c t)"))
-            T[("cB", ps)] = cB
-            T[("sB", ps)] = sB
+        def qb(ps, c0=0, cw=512):
+            if ("cB", ps) not in T:
+                T[("cB", ps)] = bpool.tile([P, 512], U32, name="cB", tag="cB", align_bytes=64)
+                T[("sB", ps)] = bpool.tile([P, 512], U8, name="sB", tag="sB", align_bytes=64)
+            cols = slice(c0, c0 + cw)
+            nc.vector.quantize_mx(out=T[("cB", ps)][:, cols].bitcast(E5), scales=T[("sB", ps)][:, cols], in_=T[("bt", ps)][:, cols, :].rearrange("q c t -> q (c t)"))
 
-        def mm0(ps, first, last):
+        def mm0(ps, first, last, js=(0, 1, 2, 3)):
             g_ = ps[1] // 4 if ps[0] == "oi" else ps[1] // 2
             key = (ps[0], ps[1] % 4 if ps[0] == "oi" else ps[1] % 2)
-            for j in range(4):
+            for j in js:
                 if first:
                     T[("acc", g_, j)] = accp.tile([P, D], F32, name="acc%d" % j, tag="acc%d" % j)
                 cols = slice(P * j, P * j + P)
@@ -308,8 +319,6 @@ def tile_lstmbaseline_pa_v_kernel(tc, x, W_ih0, b_ih0, b_hh0, a_i, a_g, a_o, gra
             if 1 <= v and v + 1 < NU:
                 v1(v + 1)
             pq = [PREP[n] for n in (2 * v - 2, 2 * v - 1) if 0 <= n < len(PREP)]
-            for key in pq:
-                prep_quant(key)
             if do1:
                 for n in range(4):
                     mm1(um, n)
@@ -324,12 +333,17 @@ def tile_lstmbaseline_pa_v_kernel(tc, x, W_ih0, b_ih0, b_hh0, a_i, a_g, a_o, gra
             if do1:
                 eo1(um, 4, "s")
                 eo1(um, 5, "s")
-            for key in pl:
-                prep_move(key, 0)
-                prep_move(key, 1)
+            if v > 0:
+                for key in pl:
+                    prep_move(key, 0)
+                    prep_move(key, 1)
             v2(v, ("sq", "ag", "c") if v == NU - 1 else ("c", "tcn", "sq", "ag"))
+            for key in pq:
+                prep_quant(key)
+            if v == NU - 1:
+                break
             for ps in bps:
-                qb(ps, 1)
+                qb(ps)
                 mm0(ps, flags(ps)[0], flags(ps)[1])
                 if flags(ps)[1]:
                     for j in range(4):
@@ -339,46 +353,64 @@ def tile_lstmbaseline_pa_v_kernel(tc, x, W_ih0, b_ih0, b_hh0, a_i, a_g, a_o, gra
                 if v % 2 == 1:
                     tr(("g", v // 2), 0)
                     tr(("g", v // 2), 1)
+                if v == 0:
+                    v1(1)
+                    s2(1)
+                    for key in pl:
+                        prep_move(key, 0)
+                        prep_move(key, 1)
                 v3(v, "o")
                 v3(v, "i")
                 tr(("oi", v), 0)
                 tr(("oi", v), 1)
                 qa(v, "g")
                 qa(v, "oi")
-                if v == 0:
-                    v1(1)
-                    s2(1)
         u = NU - 1
-        pg, po = ("g", 3), ("oi", 7)
+        pg, po, p6 = ("g", 3), ("oi", 7), ("oi", 6)
         v3(u, "g")
         tr(pg, 0)
         tr(pg, 1)
+        qb(p6)
+        mm0(p6, False, False)
         v2(u, ("tcn",))
-        v3(u, "i")
+        v3(u, "i", 0, 128)
         qa(u, "g")
         mm1(u, 4)
         mm1(u, 5)
+        v3(u, "o", 0, 128)
         eb(pg, 0, "s")
         eb(pg, 1, "s")
-        v3(u, "o")
+        v3(u, "i", 128, 128)
+        qa(u, "oi", 256, 128)
+        mm1(u, 2)
+        qa(u, "oi", 0, 128)
+        mm1(u, 0)
+        eo1(u, 4, "s")
+        eo1(u, 5, "s")
+        v3(u, "o", 128, 128)
         tr(po, 0)
         tr(po, 1)
-        qb(pg, 1)
+        qa(u, "oi", 384, 128)
+        qa(u, "oi", 128, 128)
+        qb(pg)
         mm0(pg, False, False)
-        qa(u, "oi")
-        eo1(u, 4, "s")
-        eo1(u, 5, "v")
-        mm1(u, 0)
-        mm1(u, 1)
-        eb(po, 0, "s")
-        eb(po, 1, "v")
-        qb(po, 2)
-        mm0(po, False, True)
-        mm1(u, 2)
-        mm1(u, 3)
-        eo1(u, 0, "s")
-        eo1(u, 1, "v")
-        for j in range(4):
-            eo0(1, j, "s" if j % 2 == 0 else "v")
         eo1(u, 2, "s")
-        eo1(u, 3, "v")
+        eo1(u, 0, "s")
+        eb(po, 0, "s", 0)
+        eb(po, 0, "v", 1)
+        qb(po, 0, 128)
+        eb(po, 1, "s", 0)
+        qb(po, 128, 128)
+        mm0(po, False, True, (0, 1))
+        eb(po, 1, "v", 1)
+        qb(po, 256, 128)
+        mm1(u, 3)
+        qb(po, 384, 128)
+        mm0(po, False, True, (2, 3))
+        mm1(u, 1)
+        eo0(1, 0, "s")
+        eo0(1, 1, "v")
+        eo0(1, 2, "s")
+        eo0(1, 3, "v")
+        eo1(u, 3, "s")
+        eo1(u, 1, "v")

@@ -69,7 +69,7 @@ def tile_lstmbaseline_pa_v_kernel(tc, x, W_ih0, b_ih0, b_hh0, a_i, a_g, a_o, gra
 
         def prep_load(key):
             kind, n = key
-            raw = ppool.tile([P, 4, D], BF16, name="raw", tag="raw", bufs=3)
+            raw = ppool.tile([P, 4, D], BF16, name="raw", tag="raw", bufs=4)
             if kind == "x":
                 nc.sync.dma_start(out=raw[:], in_=xv[:, n, :, :])
             elif kind == "g":
@@ -294,6 +294,8 @@ def tile_lstmbaseline_pa_v_kernel(tc, x, W_ih0, b_ih0, b_hh0, a_i, a_g, a_o, gra
 
         load_unit(0)
         load_unit(1)
+        prep_load(PREP[0])
+        prep_load(PREP[1])
         load_unit(2)
         s1(0)
         v1(0)
@@ -303,7 +305,7 @@ def tile_lstmbaseline_pa_v_kernel(tc, x, W_ih0, b_ih0, b_hh0, a_i, a_g, a_o, gra
             um = v - 1
             do1 = 4 <= um
             pl = [PREP[n] for n in (2 * v, 2 * v + 1) if n < len(PREP)]
-            for key in pl:
+            for key in [PREP[n] for n in (2 * v + 2, 2 * v + 3) if n < len(PREP)]:
                 prep_load(key)
             if v + 3 < NU:
                 load_unit(v + 3)

@@ -131,6 +131,8 @@ def tile_lstmbaseline_pa_v_kernel(tc, x, W_ih0, b_ih0, b_hh0, a_i, a_g, a_o, gra
             nc.vector.tensor_tensor(out=gg[:], in0=T[("ao", u)][:], in1=T[("gt", u // 2)][:, :, UW * wq:UW * wq + UW], op=ALU.mult)
             T[("c", u)] = c
             T[("gg", u)] = gg
+            if u in (6, 7):
+                nc.vector.tensor_tensor(out=T[("ag", u)][:], in0=T[("ag", u)][:], in1=T[("ag", u)][:], op=ALU.mult)
 
         def s2(u):
             tcn = wpool.tile([P, 4, UW], F32, name="tcn", tag="tcn")
@@ -138,7 +140,8 @@ def tile_lstmbaseline_pa_v_kernel(tc, x, W_ih0, b_ih0, b_hh0, a_i, a_g, a_o, gra
                 nc.scalar.activation(out=tcn[:, j0:j1, :], in_=T[("c", u)][:, j0:j1, :], func=ACT.Tanh, scale=-1.0)
             sq = wpool.tile([P, 4, UW], F32, name="sq", tag="sq")
             nc.scalar.activation(out=sq[:], in_=tcn[:], func=ACT.Square)
-            nc.scalar.activation(out=T[("ag", u)][:], in_=T[("ag", u)][:], func=ACT.Square)
+            if u not in (6, 7):
+                nc.scalar.activation(out=T[("ag", u)][:], in_=T[("ag", u)][:], func=ACT.Square)
             T[("tcn", u)] = tcn
             T[("sq", u)] = sq
 

from contextlib import ExitStack

import concourse.mybir as mybir
from concourse.masks import make_identity

B, D, H = 1024, 512, 1024
FLOPS = 2 * 2 * B * 3 * H * D
BYTES = B * D * 2 + 3 * H * D * 2 + 3 * B * H * 4 + B * H * 2 + B * D * 4 + 4 * H * D * 4

F32 = mybir.dt.float32
BF16 = mybir.dt.bfloat16
U32 = mybir.dt.uint32
U8 = mybir.dt.uint8
E4 = mybir.dt.float8_e4m3fn_x4
E5 = mybir.dt.float8_e5m2_x4
ACT = mybir.ActivationFunctionType
ALU = mybir.AluOpType

P = 128
UW = 256
NU = 8
ROW0 = {"i": 0, "g": 2 * H, "o": 3 * H}
WORDS = True
RUN = 2
HEAD_CUTS = 1

PREP = [("oi", 0), ("g", 0), ("oi", 1), ("oi", 2), ("g", 1), ("oi", 3), ("x", 0), ("x", 1)]


def tile_lstmbaseline_pa_v_kernel(tc, x, W_ih0, b_ih0, b_hh0, a_i, a_g, a_o, grad_out, out_0, out_1):
    nc = tc.nc
    with ExitStack() as ctx:
        const = ctx.enter_context(tc.tile_pool(name="const", bufs=1))
        apool = ctx.enter_context(tc.tile_pool(name="apool", bufs=4))
        gpool = ctx.enter_context(tc.tile_pool(name="gpool", bufs=2))
        wpool = ctx.enter_context(tc.tile_pool(name="wpool", bufs=2))
        dpool = ctx.enter_context(tc.tile_pool(name="dpool", bufs=2))
        bpool = ctx.enter_context(tc.tile_pool(name="bpool", bufs=3))
        keep = ctx.enter_context(tc.tile_pool(name="keep", bufs=1))
        ppool = ctx.enter_context(tc.tile_pool(name="ppool", bufs=2))
        spool = ctx.enter_context(tc.tile_pool(name="spool", bufs=8))
        accp = ctx.enter_context(tc.psum_pool(name="accp", bufs=1))
        work = ctx.enter_context(tc.psum_pool(name="work", bufs=4))
        ctx.enter_context(tc.manual_schedule())

        av = {
            "i": a_i.rearrange("(g p j) w -> p g j w", g=2, j=4),
            "g": a_g.rearrange("(g p j) w -> p g j w", g=2, j=4),
            "o": a_o.rearrange("(g p j) w -> p g j w", g=2, j=4),
        }
        gv = grad_out.rearrange("(g p j) w -> p g j w", g=2, j=4)
        xv = x.rearrange("(g p j) d -> p g j d", g=2, j=4)
        o0v = out_0.rearrange("(g p j) d -> p g j d", g=2, j=4)

        T = {}

        def parts(u):
            return u // 4, (u // 2) % 2, u % 2

        warm = const.tile([P, 8], F32, name="warm")
        nc.vector.memset(warm[:], 0.0)
        nc.scalar.activation(out=warm[:], in_=warm[:], func=ACT.Sigmoid)
        zero = const.tile([P, 1024], F32, name="zero")
        nc.vector.memset(zero[:], 0.0)
        identb = const.tile([P, P], BF16, name="identb")
        make_identity(nc, identb[:])
        identf = const.tile([P, P], F32, name="identf")
        make_identity(nc, identf[:])

        def prep_load(key):
            kind, n = key
            raw = ppool.tile([P, 4, D], BF16, name="raw", tag="raw", bufs=4)
            if kind == "x":
                nc.sync.dma_start(out=raw[:], in_=xv[:, n, :, :])
            elif kind == "g":
                r0 = ROW0["g"] + 512 * n
                nc.sync.dma_start(out=raw[:], in_=W_ih0[r0:r0 + 512, :].rearrange("(q t) d -> q t d", t=4))
            else:
                for s, gate in enumerate(("o", "i")):
                    r0 = ROW0[gate] + UW * n
                    nc.sync.dma_start(out=raw[64 * s:64 * s + 64, :, :], in_=W_ih0[r0:r0 + UW, :].rearrange("(q t) d -> q t d", t=4))
            T[("raw", key)] = raw

        def prep_move(key, s):
            if s == 0:
                T[("il", key)] = ppool.tile([P, 4 * D], BF16, name="il", tag="il", bufs=4, align_bytes=64)
            pp = work.tile([P, 1024], BF16, name="pp", tag="work")
            for r in range(2):
                d0 = 256 * s + 128 * r
                nc.tensor.matmul(out=pp[:, 512 * r:512 * r + 512].rearrange("p (d t) -> p d t", t=4), lhsT=identb[:], rhs=T[("raw", key)][:, :, d0:d0 + 128].rearrange("p t d -> p d t"), start=True, stop=True)
            nc.scalar.copy(out=T[("il", key)][:, 1024 * s:1024 * s + 1024], in_=pp[:])

        def prep_quant(key):
            nm = "%s%d" % key
            codes = keep.tile([P, D], U32, name="c" + nm, align_bytes=64)
            scales = keep.tile([P, D], U8, name="s" + nm, align_bytes=64)
            nc.vector.quantize_mx(out=codes[:].bitcast(E4), scales=scales[:], in_=T[("il", key)][:])
            T[("c", key)] = codes
            T[("s", key)] = scales

        def jcuts(u):
            n = HEAD_CUTS if u == 0 else 1
            return [(4 // n * s, 4 // n * s + 4 // n) for s in range(n)]

        def load_unit(u):
            g_, h, wq = parts(u)
            lo = 512 * h + UW * wq
            for gate in ("i", "g", "o"):
                T[("a" + gate, u)] = apool.tile([P, 4, UW], F32, name="a" + gate, tag="a" + gate)
            for j0, j1 in jcuts(u):
                for gate in ("i", "g"):
                    nc.sync.dma_start(out=T[("a" + gate, u)][:, j0:j1, :], in_=av[gate][:, g_, j0:j1, lo:lo + UW])
            nc.sync.dma_start(out=T[("ao", u)][:], in_=av["o"][:, g_, :, lo:lo + UW])
            if wq == 0:
                gt = gpool.tile([P, 4, 512], BF16, name="gt", tag="gt")
                nc.sync.dma_start(out=gt[:], in_=gv[:, g_, :, 512 * h:512 * h + 512])
                T[("gt", u // 2)] = gt

        def s1(u):
            for j0, j1 in jcuts(u):
                nc.scalar.activation(out=T[("ai", u)][:, j0:j1, :], in_=T[("ai", u)][:, j0:j1, :], func=ACT.Sigmoid)
                nc.scalar.activation(out=T[("ag", u)][:, j0:j1, :], in_=T[("ag", u)][:, j0:j1, :], func=ACT.Tanh)
            nc.scalar.activation(out=T[("ao", u)][:], in_=T[("ao", u)][:], func=ACT.Sigmoid)

        def v1(u):
            wq = u % 2
            c = wpool.tile([P, 4, UW], F32, name="c", tag="c")
            for j0, j1 in jcuts(u):
                nc.vector.tensor_tensor(out=c[:, j0:j1, :], in0=T[("ai", u)][:, j0:j1, :], in1=T[("ag", u)][:, j0:j1, :], op=ALU.mult)
            gg = wpool.tile([P, 4, UW], F32, name="gg", tag="gg")
            nc.vector.tensor_tensor(out=gg[:], in0=T[("ao", u)][:], in1=T[("gt", u // 2)][:, :, UW * wq:UW * wq + UW], op=ALU.mult)
            T[("c", u)] = c
            T[("gg", u)] = gg
            if u in (6, 7):
                nc.vector.tensor_tensor(out=T[("ag", u)][:], in0=T[("ag", u)][:], in1=T[("ag", u)][:], op=ALU.mult)

        def s2(u):
            tcn = wpool.tile([P, 4, UW], F32, name="tcn", tag="tcn")
            for j0, j1 in jcuts(u):
                nc.scalar.activation(out=tcn[:, j0:j1, :], in_=T[("c", u)][:, j0:j1, :], func=ACT.Tanh, scale=-1.0)
            sq = wpool.tile([P, 4, UW], F32, name="sq", tag="sq")
            nc.scalar.activation(out=sq[:], in_=tcn[:], func=ACT.Square)
            if u not in (6, 7):
                nc.scalar.activation(out=T[("ag", u)][:], in_=T[("ag", u)][:], func=ACT.Square)
            T[("tcn", u)] = tcn
            T[("sq", u)] = sq

        def stt(out, in0, in1):
            nc.vector.scalar_tensor_tensor(out=out, in0=in0, scalar=1.0, in1=in1, op0=ALU.subtract, op1=ALU.mult)

        def v2(u, names):
            for nm in names:
                if nm == "c":
                    stt(T[("c", u)][:], T[("ai", u)][:], T[("c", u)][:])
                elif nm == "tcn":
                    stt(T[("tcn", u)][:], T[("ao", u)][:], T[("tcn", u)][:])
                elif nm == "sq":
                    stt(T[("sq", u)][:], T[("sq", u)][:], T[("gg", u)][:])
                else:
                    stt(T[("ag", u)][:], T[("ag", u)][:], T[("ai", u)][:])

        FACT = {"o": ("tcn", "gg"), "i": ("c", "sq"), "g": ("ag", "sq")}

        def v3(u, gate, f0=0, fw=UW):
            k, wq = u // 2, u % 2
            if gate == "g":
                if wq == 0:
                    T[("da", "g", k)] = dpool.tile([P, 512, 4], BF16, name="dag", tag="dag", align_bytes=64)
                da, lo = T[("da", "g", k)], UW * wq
            else:
                if ("da", "oi", u) not in T:
                    T[("da", "oi", u)] = dpool.tile([P, 512, 4], BF16, name="daoi", tag="daoi", align_bytes=64)
                da, lo = T[("da", "oi", u)], (0 if gate == "o" else UW)
            n0, n1 = FACT[gate]
            nc.vector.tensor_tensor(
                out=da[:, lo + f0:lo + f0 + fw, :].rearrange("p (c i) j -> p c j i", i=RUN),
                in0=T[(n0, u)][:, :, f0:f0 + fw].rearrange("p j (c i) -> p c j i", i=RUN),
                in1=T[(n1, u)][:, :, f0:f0 + fw].rearrange("p j (c i) -> p c j i", i=RUN),
                op=ALU.mult,
            )

        def qa(u, kind, c0=0, cw=512):
            k, wq = u // 2, u % 2
            if kind == "oi":
                if ("cA", "oi", u) not in T:
                    T[("cA", "oi", u)] = keep.tile([P, 512], U32, name="cAoi%d" % u, align_bytes=64)
                    T[("sA", "oi", u)] = keep.tile([P, 512], U8, name="sAoi%d" % u, align_bytes=64)
                n, cols = u, slice(c0, c0 + cw)
            else:
                if wq == 0:
                    T[("cA", "g", k)] = keep.tile([P, 512], U32, name="cAg%d" % k, align_bytes=64)
                    T[("sA", "g", k)] = keep.tile([P, 512], U8, name="sAg%d" % k, align_bytes=64)
                n, cols = k, slice(UW * wq, UW * wq + UW)
            nc.vector.quantize_mx(
                out=T[("cA", kind, n)][:, cols].bitcast(E5),
                scales=T[("sA", kind, n)][:, cols],
                in_=T[("da", kind, n)][:, cols, :].rearrange("p w j -> p (w j)"),
            )

        def tr(ps, s):
            da = T[("da", ps[0], ps[1])]
            if WORDS:
                words = da[:].rearrange("p w j -> p (w j)").bitcast(F32).rearrange("p (q r) -> p q r", r=8)
                tp = work.tile([P, 4, P], F32, name="tp", tag="work")
                for t in range(4):
                    nc.tensor.transpose(out=tp[:, t, :], in_=words[:, :, 2 * t + s], identity=identf[:])
            else:
                view = da[:].rearrange("p (q t) j -> p q t j", t=4)
                tp = work.tile([P, 4, 256], BF16, name="tp", tag="work")
                for j2 in range(2):
                    for t in range(4):
                        nc.tensor.transpose(out=tp[:, t, P * j2:P * j2 + P], in_=view[:, :, t, 2 * s + j2], identity=identb[:])
            T[("tp", ps, s)] = tp

        def eb(ps, s, eng, par=None):
            if ("bt", ps) not in T:
                T[("bt", ps)] = bpool.tile([P, 512, 4], BF16, name="bt", tag="bt", align_bytes=64)
            if WORDS:
                dst = T[("bt", ps)][:, 256 * s:256 * s + 256, :].rearrange("q (e c) t -> q e c t", e=2)
                src = T[("tp", ps, s)][:].rearrange("q t c -> q (t c)").bitcast(BF16).rearrange("q (t c e) -> q e c t", t=4, e=2)
                if par is not None:
                    dst = dst[:, par, :, :]
                    src = src[:, par, :, :]
            else:
                dst = T[("bt", ps)][:, 256 * s:256 * s + 256, :]
                src = T[("tp", ps, s)][:].rearrange("q t c -> q c t")
            if eng == "v":
                nc.vector.tensor_copy(out=dst, in_=src)
            else:
                nc.scalar.copy(out=dst, in_=src)

        def qb(ps, c0=0, cw=512):
            if ("cB", ps) not in T:
                T[("cB", ps)] = bpool.tile([P, 512], U32, name="cB", tag="cB", align_bytes=64)
                T[("sB", ps)] = bpool.tile([P, 512], U8, name="sB", tag="sB", align_bytes=64)
            cols = slice(c0, c0 + cw)
            nc.vector.quantize_mx(out=T[("cB", ps)][:, cols].bitcast(E5), scales=T[("sB", ps)][:, cols], in_=T[("bt", ps)][:, cols, :].rearrange("q c t -> q (c t)"))

        def mm0(ps, first, last, js=(0, 1, 2, 3)):
            g_ = ps[1] // 4 if ps[0] == "oi" else ps[1] // 2
            key = (ps[0], ps[1] % 4 if ps[0] == "oi" else ps[1] % 2)
            for j in js:
                if first:
                    T[("acc", g_, j)] = accp.tile([P, D], F32, name="acc%d" % j, tag="acc%d" % j)
                cols = slice(P * j, P * j + P)
                nc.tensor.matmul_mx(
                    out=T[("acc", g_, j)][:],
                    lhsT=T[("cB", ps)][:, cols].bitcast(E5), lhsT_scale=T[("sB", ps)][:, cols],
                    rhs=T[("c", key)][:].bitcast(E4), rhs_scale=T[("s", key)][:],
                    start=first, stop=last,
                )

        def evac(src, dst_dram, eng):
            st = spool.tile([P, D], F32, name="st", tag="st")
            if eng == "v":
                nc.vector.tensor_copy(out=st[:], in_=src)
            else:
                nc.scalar.copy(out=st[:], in_=src)
            nc.sync.dma_start(out=dst_dram, in_=st[:])

        def eo0(g_, j, eng):
            evac(T[("acc", g_, j)][:], o0v[:, g_, j, :], eng)

        def mm1(u, n):
            g_, h, wq = parts(u)
            acc = work.tile([P, D], F32, name="o1", tag="work")
            for gg_ in range(2):
                if n < 4:
                    kind, idx, c0 = "oi", 4 * gg_ + u % 4, P * n
                else:
                    kind, idx, c0 = "g", 2 * gg_ + h, UW * wq + P * (n - 4)
                cols = slice(c0, c0 + P)
                key = ("x", gg_)
                nc.tensor.matmul_mx(
                    out=acc[:],
                    lhsT=T[("cA", kind, idx)][:, cols].bitcast(E5), lhsT_scale=T[("sA", kind, idx)][:, cols],
                    rhs=T[("c", key)][:].bitcast(E4), rhs_scale=T[("s", key)][:],
                    start=(gg_ == 0), stop=(gg_ == 1),
                )
            T[("o1", u, n)] = acc

        def eo1(u, n, eng):
            g_, h, wq = parts(u)
            gate = ("o", "i", "g")[n // 2]
            r0 = ROW0[gate] + 512 * h + UW * wq + P * (n % 2)
            evac(T[("o1", u, n)][:], out_1[r0:r0 + P, :], eng)

        def passes_of(u):
            if u % 2 == 0:
                return [("oi", u)]
            return [("g", u // 2), ("oi", u)]

        def flags(ps):
            first = ps[0] == "oi" and ps[1] % 4 == 0
            last = ps[0] == "oi" and ps[1] % 4 == 3
            return first, last

        load_unit(0)
        load_unit(1)
        prep_load(PREP[0])
        prep_load(PREP[1])
        load_unit(2)
        s1(0)
        v1(0)
        s2(0)
        s1(1)
        for v in range(0, NU):
            um = v - 1
            do1 = 4 <= um
            pl = [PREP[n] for n in (2 * v, 2 * v + 1) if n < len(PREP)]
            for key in [PREP[n] for n in (2 * v + 2, 2 * v + 3) if n < len(PREP)]:
                prep_load(key)
            if v + 3 < NU:
                load_unit(v + 3)
            if v == 2:
                for z in range(4):
                    nc.sync.dma_start(out=out_1[H + 256 * z:H + 256 * z + 256, :].rearrange("(p r) d -> p (r d)", r=2), in_=zero[:])
            bps = passes_of(um) if um >= 0 else []
            for ps in bps:
                eb(ps, 0, "s")
                eb(ps, 1, "s")
            if v + 2 < NU:
                s1(v + 2)
            if 1 <= v and v + 1 < NU:
                v1(v + 1)
            pq = [PREP[n] for n in (2 * v - 2, 2 * v - 1) if 0 <= n < len(PREP)]
            if do1:
                for n in range(4):
                    mm1(um, n)
                eo1(um, 0, "s")
                eo1(um, 1, "s")
                mm1(um, 4)
                mm1(um, 5)
                eo1(um, 2, "s")
                eo1(um, 3, "s")
            if 1 <= v and v + 1 < NU:
                s2(v + 1)
            if do1:
                eo1(um, 4, "s")
                eo1(um, 5, "s")
            if v > 0:
                for key in pl:
                    prep_move(key, 0)
                    prep_move(key, 1)
            v2(v, ("sq", "ag", "c") if v == NU - 1 else ("c", "tcn", "sq", "ag"))
            for key in pq:
                prep_quant(key)
            if v == NU - 1:
                break
            for ps in bps:
                qb(ps)
                mm0(ps, flags(ps)[0], flags(ps)[1])
                if flags(ps)[1]:
                    for j in range(4):
                        eo0(ps[1] // 4, j, "s")
            if v < NU - 1:
                v3(v, "g")
                if v % 2 == 1:
                    tr(("g", v // 2), 0)
                    tr(("g", v // 2), 1)
                if v == 0:
                    v1(1)
                    s2(1)
                    for key in pl:
                        prep_move(key, 0)
                        prep_move(key, 1)
                v3(v, "o")
                v3(v, "i")
                tr(("oi", v), 0)
                tr(("oi", v), 1)
                qa(v, "g")
                qa(v, "oi")
        u = NU - 1
        pg, po, p6 = ("g", 3), ("oi", 7), ("oi", 6)
        v3(u, "g")
        tr(pg, 0)
        tr(pg, 1)
        qb(p6)
        mm0(p6, False, False)
        v2(u, ("tcn",))
        v3(u, "i", 0, 128)
        qa(u, "g")
        mm1(u, 4)
        mm1(u, 5)
        v3(u, "o", 0, 128)
        eb(pg, 0, "s")
        eb(pg, 1, "s")
        v3(u, "i", 128, 128)
        qa(u, "oi", 256, 128)
        mm1(u, 2)
        qa(u, "oi", 0, 128)
        mm1(u, 0)
        eo1(u, 4, "s")
        eo1(u, 5, "s")
        v3(u, "o", 128, 128)
        tr(po, 0)
        tr(po, 1)
        qa(u, "oi", 384, 128)
        qa(u, "oi", 128, 128)
        qb(pg)
        mm0(pg, False, False)
        eo1(u, 2, "s")
        eo1(u, 0, "s")
        eb(po, 0, "s", 0)
        eb(po, 0, "v", 1)
        qb(po, 0, 128)
        eb(po, 1, "s", 0)
        qb(po, 128, 128)
        mm0(po, False, True, (0, 1))
        eb(po, 1, "v", 1)
        qb(po, 256, 128)
        mm1(u, 3)
        qb(po, 384, 128)
        mm0(po, False, True, (2, 3))
        mm1(u, 1)
        eo0(1, 0, "s")
        eo0(1, 1, "v")
        eo0(1, 2, "s")
        eo0(1, 3, "v")
        eo1(u, 3, "s")
        eo1(u, 1, "v")
